import numpy as np
import ml_dtypes


def mxq(x, axis, fmt="e4m3"):
    dtype, down = {"e4m3": (ml_dtypes.float8_e4m3fn, 7), "e5m2": (ml_dtypes.float8_e5m2, 14)}[fmt]
    v = np.moveaxis(np.asarray(x, np.float32).astype(ml_dtypes.bfloat16).astype(np.float64), axis, -1)
    blocks = v.reshape(v.shape[:-1] + (-1, 32))
    amax = np.abs(blocks).max(-1, keepdims=True)
    byte = np.maximum(np.where(amax > 0, np.frexp(amax)[1] - 1 + 127, 0) - down, 1)
    scale = np.exp2(byte - 127.0)
    codes = (blocks / scale).astype(np.float32).astype(dtype).astype(np.float64)
    return np.moveaxis((codes * scale).reshape(v.shape), -1, axis)


WIDE = False


def mx_kscale(k):
    if not WIDE:
        return np.ones(k)
    levels = np.array([10, -10, 5, -5, 0])
    a = np.random.permutation(np.resize(levels, k // 512 * 4)).reshape(k // 512, 4)
    idx = np.arange(k)
    return np.exp2(a[idx // 512, idx % 128 // 32])


BF16 = ml_dtypes.bfloat16


def bf(x):
    return np.asarray(x, np.float32).astype(BF16)


def f64(x):
    return np.asarray(x).astype(np.float64)


B, C, M, O, H, W = 4, 512, 512, 512, 32, 32
H2, W2 = H // 2, W // 2
KS = 3
PAD = KS // 2
BN_EPS = 1e-5


def haar_ll(x):
    a = x[:, :, 0::2, 0::2]
    b = x[:, :, 0::2, 1::2]
    c = x[:, :, 1::2, 0::2]
    d = x[:, :, 1::2, 1::2]
    return (a + b + c + d) * 0.5


def windows(u):
    up = np.pad(u, ((0, 0), (0, 0), (PAD, PAD), (PAD, PAD)))
    return np.stack([up[:, :, i:i + H2, j:j + W2] for i in range(KS) for j in range(KS)], axis=-1)


def setup_inputs():
    s, t = mx_kscale(C), mx_kscale(M)
    return {
        "x": bf(np.random.standard_normal((B, C, H, W)) * s[None, :, None, None]),
        "w_c1": bf(np.random.standard_normal((M, C)) / np.sqrt(C) * t[:, None] / s[None, :]),
        "b_c1": bf(np.random.standard_normal(M) * 0.3 * t),
        "w_q": bf(np.random.standard_normal((O, M)) / np.sqrt(M) / t[None, :]),
        "w_k": bf(np.random.standard_normal((O, M)) / np.sqrt(M) / t[None, :]),
        "w_v": bf(np.random.standard_normal((O, M)) / np.sqrt(M) / t[None, :]),
        "bn_gamma": bf(1.0 + 0.1 * np.random.standard_normal(O)),
        "bn_beta": bf(0.3 * np.random.standard_normal(O)),
        "prelu_a": bf(np.random.uniform(0.15, 0.35, (1,))),
    }


def reference(x, w_c1, b_c1, w_q, w_k, w_v, bn_gamma, bn_beta, prelu_a):
    ll = haar_ll(f64(x)).reshape(B, C, H2 * W2)
    y = (mxq(f64(w_c1), 1, "e4m3") @ mxq(ll, 1, "e4m3")) + f64(b_c1)[None, :, None]
    yq = mxq(y, 1, "e4m3")
    q = (mxq(f64(w_q), 1, "e4m3") @ yq).reshape(B, O, H2, W2)
    k = (mxq(f64(w_k), 1, "e4m3") @ yq).reshape(B, O, H2, W2)
    v = (mxq(f64(w_v), 1, "e4m3") @ yq).reshape(B, O, H2, W2)
    kw = windows(k)
    vw = windows(v)
    z = q[..., None] * kw
    e = np.exp(z - z.max(-1, keepdims=True))
    attn = e / e.sum(-1, keepdims=True)
    att = (attn * vw).sum(-1)
    m = att.mean(axis=(0, 2, 3), keepdims=True)
    var = att.var(axis=(0, 2, 3), keepdims=True)
    n = f64(bn_gamma)[None, :, None, None] * (att - m) / np.sqrt(var + BN_EPS) + f64(bn_beta)[None, :, None, None]
    return np.where(n >= 0, n, f64(prelu_a) * n)

@@ -1,0 +1,327 @@
+import concourse.mybir as mybir
+from concourse.masks import make_identity
+
+F32 = mybir.dt.float32
+BF16 = mybir.dt.bfloat16
+U32 = mybir.dt.uint32
+U8 = mybir.dt.uint8
+FP8X4 = mybir.dt.float8_e4m3fn_x4
+ALU = mybir.AluOpType
+ACT = mybir.ActivationFunctionType
+
+P = 128
+PACK = 4
+IMAGES = 4
+CHANNELS = 512
+SIDE = 16
+PIX = SIDE * SIDE
+PAIR = 2
+CHUNK = PAIR * PIX
+TILES = CHANNELS // P
+SHIFTS = (-1, 0, 1)
+TAPS = len(SHIFTS) * len(SHIFTS)
+BLOCKS = CHUNK // P
+BN_EPS = 1e-5
+BN_COUNT = IMAGES * PIX
+
+FLOPS = 4 * 2 * CHANNELS * CHANNELS * IMAGES * PIX
+
+
+def inside(shift):
+    return max(0, -shift), SIDE - max(0, shift)
+
+
+def tile_merge_pa_kernel(
+    tc, x, w_c1, b_c1, w_q, w_k, w_v, bn_gamma, bn_beta, prelu_a, out
+):
+    nc = tc.nc
+    weights = {"c1": w_c1, "q": w_q, "k": w_k, "v": w_v}
+
+    with tc.tile_pool(name="keep", bufs=1) as keep:
+        ident = keep.tile([P, P], F32)
+        make_identity(nc, ident[:])
+
+        w_codes = {}
+        w_scales = {}
+        for name in weights:
+            w_codes[name] = keep.tile([P, CHANNELS], U32, name="codes_" + name, align_bytes=64)
+            w_scales[name] = keep.tile([P, CHANNELS], U8, name="scales_" + name, align_bytes=64)
+        y_codes = keep.tile([P, IMAGES * PIX], U32, align_bytes=64)
+        y_scales = keep.tile([P, IMAGES * PIX], U8, align_bytes=64)
+
+        z = keep.tile([P, len(SHIFTS), len(SHIFTS), PAIR, SIDE, SIDE], F32)
+        pv = keep.tile([P, len(SHIFTS), len(SHIFTS), PAIR, SIDE, SIDE], F32)
+        for planes in (z, pv):
+            nc.vector.memset(planes[:, 0, :, :, 0, :], 0.0)
+            nc.vector.memset(planes[:, 2, :, :, SIDE - 1, :], 0.0)
+            nc.vector.memset(planes[:, :, 0, :, :, 0], 0.0)
+            nc.vector.memset(planes[:, :, 2, :, :, SIDE - 1], 0.0)
+
+        bias_c1 = keep.tile([P, PACK], F32)
+        gamma_pm = keep.tile([P, TILES, 2], F32)
+        beta_pm = keep.tile([P, TILES, 2], F32)
+        minus_slope = keep.tile([P, 1], F32)
+        eps = keep.tile([P, 1], F32)
+        nc.vector.memset(eps[:], BN_EPS)
+
+        with tc.tile_pool(name="head", bufs=2) as head, tc.psum_pool(name="head_banks", bufs=4) as head_banks:
+            x_sb = []
+            w_raw = {}
+
+            def load_image(b):
+                x_sb.append(head.tile([P, PACK * 4 * PIX], BF16, name="x%d" % b, bufs=1))
+                nc.sync.dma_start(
+                    out=x_sb[b][:].rearrange("p (u f) -> p u f", u=2),
+                    in_=x[b].rearrange("(u p e) h w -> p u (e h w)", u=2, e=2),
+                )
+
+            def load_weight(name, runs, rows):
+                w_raw[name] = head.tile([P, TILES * CHANNELS], BF16, name="raw_" + name, bufs=1)
+                nc.sync.dma_start(out=w_raw[name][:].rearrange("r (u f) -> r u f", u=runs), in_=rows)
+
+            load_image(0)
+            load_weight("c1", 2, w_c1.rearrange("(u r e) c -> r u (e c)", u=2, e=2))
+            for b in range(1, IMAGES):
+                load_image(b)
+            for name in ("q", "k", "v"):
+                load_weight(name, 1, weights[name].rearrange("(r u a) m -> r u (a m)", u=1, a=TILES))
+
+            b1_bf = head.tile([P, PACK], BF16, bufs=1)
+            nc.scalar.dma_start(
+                out=b1_bf[:].rearrange("r (u e) -> r u e", u=2),
+                in_=b_c1.rearrange("(u r e) -> r u e", u=2, e=2),
+            )
+            gamma_bf = head.tile([P, TILES], BF16, bufs=1)
+            nc.scalar.dma_start(out=gamma_bf[:], in_=bn_gamma.rearrange("(r a) -> r a", a=TILES))
+            beta_bf = head.tile([P, TILES], BF16, bufs=1)
+            nc.scalar.dma_start(out=beta_bf[:], in_=bn_beta.rearrange("(r a) -> r a", a=TILES))
+            slope_bf = head.tile([P, 1], BF16, bufs=1)
+            nc.scalar.dma_start(out=slope_bf[:], in_=prelu_a.partition_broadcast(P))
+
+            nc.vector.tensor_copy(out=bias_c1[:], in_=b1_bf[:])
+            nc.vector.tensor_copy(out=gamma_pm[:, :, 0], in_=gamma_bf[:])
+            nc.vector.tensor_scalar_mul(out=gamma_pm[:, :, 1], in0=gamma_bf[:], scalar1=-1.0)
+            nc.vector.tensor_copy(out=beta_pm[:, :, 0], in_=beta_bf[:])
+            nc.vector.tensor_scalar_mul(out=beta_pm[:, :, 1], in0=beta_bf[:], scalar1=-1.0)
+            nc.vector.tensor_scalar_mul(out=minus_slope[:], in0=slope_bf[:], scalar1=-1.0)
+
+            def quantise_weight(name):
+                words = w_raw[name][:].bitcast(F32)
+                grouped = head.tile([P, TILES * P * PACK], BF16, tag="grouped", align_bytes=64)
+                grouped_words = grouped[:].bitcast(F32).rearrange("p (a r u) -> p a r u", a=TILES, u=2)
+                for first in range(0, TILES, 2):
+                    turned = head_banks.tile([P, 2, 2, P], F32, tag="turned")
+                    for a in range(2):
+                        for u in range(2):
+                            col = ((first + a) * 2 + u) * P
+                            nc.tensor.transpose(turned[:, a, u, :], words[:, col : col + P], ident[:])
+                    nc.scalar.copy(
+                        out=grouped_words[:, first : first + 2],
+                        in_=turned[:].rearrange("p a u r -> p a r u"),
+                    )
+                nc.vector.quantize_mx(
+                    out=w_codes[name][:].bitcast(FP8X4), scales=w_scales[name][:], in_=grouped[:]
+                )
+
+            quantise_weight("c1")
+
+            ll_codes = head.tile([P, IMAGES * PIX], U32, bufs=1, align_bytes=64)
+            ll_scales = head.tile([P, IMAGES * PIX], U8, bufs=1, align_bytes=64)
+            for b in range(IMAGES):
+                row_pairs = x_sb[b][:].rearrange("p (r two w) -> p r two w", two=2, w=2 * SIDE)
+                row_sums = head.tile([P, PACK * PIX * 2], F32, tag="row_sums")
+                nc.vector.tensor_tensor(
+                    out=row_sums[:].rearrange("p (r w) -> p r w", w=2 * SIDE),
+                    in0=row_pairs[:, :, 0, :],
+                    in1=row_pairs[:, :, 1, :],
+                    op=ALU.add,
+                )
+                col_pairs = row_sums[:].rearrange("p (t x two) -> p x t two", t=PACK, two=2)
+                ll2 = head.tile([P, PIX, PACK], BF16, tag="ll2", align_bytes=64)
+                nc.vector.tensor_tensor(
+                    out=ll2[:], in0=col_pairs[:, :, :, 0], in1=col_pairs[:, :, :, 1], op=ALU.add
+                )
+                cols = slice(b * PIX, (b + 1) * PIX)
+                nc.vector.quantize_mx(
+                    out=ll_codes[:, cols].bitcast(FP8X4),
+                    scales=ll_scales[:, cols],
+                    in_=ll2[:].rearrange("p x t -> p (x t)"),
+                )
+
+            for name in ("q", "k", "v"):
+                quantise_weight(name)
+
+            y_bf = head.tile([P, IMAGES * PIX, PACK], BF16, bufs=1, align_bytes=64)
+            for g in range(IMAGES * PIX // P):
+                cols = slice(g * P, (g + 1) * P)
+                y_bank = head_banks.tile([P, PACK, P], F32, tag="y_bank")
+                for t in range(PACK):
+                    rows = slice(t * P, (t + 1) * P)
+                    nc.tensor.matmul_mx(
+                        out=y_bank[:, t, :],
+                        lhsT=w_codes["c1"][:, rows].bitcast(FP8X4),
+                        lhsT_scale=w_scales["c1"][:, rows],
+                        rhs=ll_codes[:, cols].bitcast(FP8X4),
+                        rhs_scale=ll_scales[:, cols],
+                        start=True,
+                        stop=True,
+                    )
+                nc.vector.scalar_tensor_tensor(
+                    out=y_bf[:, cols, :],
+                    in0=y_bank[:].rearrange("p t x -> p x t"),
+                    scalar=0.5,
+                    in1=bias_c1[:].unsqueeze(1).to_broadcast([P, P, PACK]),
+                    op0=ALU.mult,
+                    op1=ALU.add,
+                )
+            for h in range(IMAGES // PAIR):
+                cols = slice(h * CHUNK, (h + 1) * CHUNK)
+                nc.vector.quantize_mx(
+                    out=y_codes[:, cols].bitcast(FP8X4),
+                    scales=y_scales[:, cols],
+                    in_=y_bf[:, cols, :].rearrange("p x t -> p (x t)"),
+                )
+
+        z_planes = z[:].rearrange("p s t b i j -> p (s t) b (i j)")
+        pv_blocks = pv[:].rearrange("p s t b (f i) j -> p (s t) (b f) (i j)", f=2)
+        out_tiles = out.rearrange("b (r a) h w -> a r b (h w)", a=TILES)
+
+        with tc.tile_pool(name="work", bufs=2) as work, tc.psum_pool(name="banks", bufs=1) as banks:
+
+            def project(name, a, h):
+                bank = banks.tile([P, PAIR, SIDE, SIDE], F32, tag="bank_" + name)
+                rows = slice(a * P, (a + 1) * P)
+                cols = slice(h * CHUNK, (h + 1) * CHUNK)
+                nc.tensor.matmul_mx(
+                    out=bank[:].rearrange("p b i j -> p (b i j)"),
+                    lhsT=w_codes[name][:, rows].bitcast(FP8X4),
+                    lhsT_scale=w_scales[name][:, rows],
+                    rhs=y_codes[:, cols].bitcast(FP8X4),
+                    rhs_scale=y_scales[:, cols],
+                    start=True,
+                    stop=True,
+                )
+                return bank
+
+            def sum_planes(blocks, tag):
+                total = banks.tile([P, BLOCKS, P], F32, tag=tag)
+                for g in range(BLOCKS):
+                    for d in range(TAPS):
+                        nc.tensor.matmul(
+                            out=total[:, g, :],
+                            lhsT=blocks[:, d, g, :],
+                            rhs=ident[:],
+                            is_transpose=True,
+                            start=(d == 0),
+                            stop=(d == TAPS - 1),
+                        )
+                return total
+
+            def window_attention(a, h, att, att_sum):
+                q_bank = project("q", a, h)
+                k_bank = project("k", a, h)
+                v_bank = project("v", a, h)
+                q_sb = work.tile([P, PAIR, SIDE, SIDE], F32, tag="q_sb")
+                nc.scalar.copy(out=q_sb[:], in_=q_bank[:])
+
+                for s, di in enumerate(SHIFTS):
+                    i0, i1 = inside(di)
+                    for t, dj in enumerate(SHIFTS):
+                        j0, j1 = inside(dj)
+                        nc.vector.tensor_tensor(
+                            out=z[:, s, t, :, i0:i1, j0:j1],
+                            in0=k_bank[:, :, i0 + di : i1 + di, j0 + dj : j1 + dj],
+                            in1=q_sb[:, :, i0:i1, j0:j1],
+                            op=ALU.mult,
+                        )
+
+                top = work.tile([P, 4, PAIR, PIX], F32, tag="top")
+                z_max = work.tile([P, PAIR, PIX], F32, tag="z_max")
+                for b in range(PAIR):
+                    nc.vector.tensor_max(out=top[:, :, b], in0=z_planes[:, 0:4, b], in1=z_planes[:, 4:8, b])
+                for b in range(PAIR):
+                    nc.vector.tensor_max(out=top[:, 0:2, b], in0=top[:, 0:2, b], in1=top[:, 2:4, b])
+                for b in range(PAIR):
+                    nc.vector.tensor_max(out=top[:, 0, b], in0=top[:, 0, b], in1=top[:, 1, b])
+                for b in range(PAIR):
+                    nc.vector.tensor_max(out=z_max[:, b], in0=top[:, 0, b], in1=z_planes[:, 8, b])
+
+                e = work.tile([P, TAPS, PAIR, PIX], F32, tag="e")
+                for b in range(PAIR):
+                    nc.vector.tensor_tensor(
+                        out=e[:, :, b],
+                        in0=z_planes[:, :, b],
+                        in1=z_max[:, b].unsqueeze(1).to_broadcast([P, TAPS, PIX]),
+                        op=ALU.subtract,
+                    )
+                    nc.scalar.activation(out=e[:, :, b], in_=e[:, :, b], func=ACT.Exp)
+
+                den_t = sum_planes(e[:].rearrange("p d b (f x) -> p d (b f) x", f=2), "den_t")
+                ln_den = work.tile([P, BLOCKS, P], F32, tag="ln_den")
+                nc.scalar.activation(out=ln_den[:], in_=den_t[:], func=ACT.Ln)
+                r_den = work.tile([P, BLOCKS, P], F32, tag="r_den")
+                nc.scalar.activation(out=r_den[:], in_=ln_den[:], func=ACT.Exp, scale=-1.0)
+
+                e_maps = e[:].rearrange("p (s t) b (i j) -> p s t b i j", s=len(SHIFTS), i=SIDE)
+                for s, di in enumerate(SHIFTS):
+                    i0, i1 = inside(di)
+                    for t, dj in enumerate(SHIFTS):
+                        j0, j1 = inside(dj)
+                        nc.vector.tensor_tensor(
+                            out=pv[:, s, t, :, i0:i1, j0:j1],
+                            in0=v_bank[:, :, i0 + di : i1 + di, j0 + dj : j1 + dj],
+                            in1=e_maps[:, s, t, :, i0:i1, j0:j1],
+                            op=ALU.mult,
+                        )
+                num_t = sum_planes(pv_blocks, "num_t")
+
+                att_t = work.tile([P, BLOCKS, P], F32, tag="att_t")
+                nc.vector.tensor_mul(out=att_t[:], in0=num_t[:], in1=r_den[:])
+                att_bank = banks.tile([P, BLOCKS, P], F32, tag="att_bank")
+                for g in range(BLOCKS):
+                    nc.tensor.transpose(att_bank[:, g, :], att_t[:, g, :], ident[:])
+                nc.scalar.activation(
+                    out=att, in_=att_bank[:].rearrange("p g x -> p (g x)"), func=ACT.Copy, accum_out=att_sum
+                )
+
+            for a in range(TILES):
+                att = work.tile([P, IMAGES * PIX], F32, tag="att")
+                att_sums = work.tile([P, IMAGES // PAIR], F32, tag="att_sums")
+                for h in range(IMAGES // PAIR):
+                    window_attention(a, h, att[:, h * CHUNK : (h + 1) * CHUNK], att_sums[:, h : h + 1])
+
+                minus_mean = work.tile([P, 1], F32, tag="minus_mean")
+                nc.vector.tensor_scalar(
+                    out=minus_mean[:],
+                    in0=att_sums[:, 0:1],
+                    scalar1=att_sums[:, 1:2],
+                    scalar2=-1.0 / BN_COUNT,
+                    op0=ALU.add,
+                    op1=ALU.mult,
+                )
+                squares = work.tile([P, IMAGES * PIX], F32, tag="squares")
+                sum_squares = work.tile([P, 1], F32, tag="sum_squares")
+                nc.scalar.activation(
+                    out=squares[:], in_=att[:], func=ACT.Square, bias=minus_mean[:], accum_out=sum_squares[:]
+                )
+                ln_var = work.tile([P, 1], F32, tag="ln_var")
+                nc.scalar.activation(
+                    out=ln_var[:], in_=sum_squares[:], func=ACT.Ln, scale=1.0 / BN_COUNT, bias=eps[:]
+                )
+                r_std = work.tile([P, 1], F32, tag="r_std")
+                nc.scalar.activation(out=r_std[:], in_=ln_var[:], func=ACT.Exp, scale=-0.5)
+                gain = work.tile([P, 2], F32, tag="gain")
+                nc.vector.tensor_scalar_mul(out=gain[:], in0=gamma_pm[:, a, :], scalar1=r_std[:])
+                shift = work.tile([P, 2], F32, tag="shift")
+                nc.vector.scalar_tensor_tensor(
+                    out=shift[:], in0=gain[:], scalar=minus_mean[:], in1=beta_pm[:, a, :], op0=ALU.mult, op1=ALU.add
+                )
+                above = work.tile([P, IMAGES * PIX], F32, tag="above")
+                nc.scalar.activation(out=above[:], in_=att[:], func=ACT.Relu, scale=gain[:, 0:1], bias=shift[:, 0:1])
+                below = work.tile([P, IMAGES * PIX], F32, tag="below")
+                nc.scalar.activation(out=below[:], in_=att[:], func=ACT.Relu, scale=gain[:, 1:2], bias=shift[:, 1:2])
+                result = work.tile([P, IMAGES * PIX], F32, tag="result")
+                nc.vector.scalar_tensor_tensor(
+                    out=result[:], in0=below[:], scalar=minus_slope[:], in1=above[:], op0=ALU.mult, op1=ALU.add
+                )
+                nc.sync.dma_start(out=out_tiles[a], in_=result[:].rearrange("p (b x) -> p b x", b=IMAGES))

@@ -49,9 +49,10 @@ def tile_merge_pa_kernel(
         y_codes = keep.tile([P, IMAGES * PIX], U32, align_bytes=64)
         y_scales = keep.tile([P, IMAGES * PIX], U8, align_bytes=64)
 
-        z = keep.tile([P, len(SHIFTS), len(SHIFTS), PAIR, SIDE, SIDE], F32)
+        z_even = keep.tile([P, len(SHIFTS), len(SHIFTS), PAIR, SIDE, SIDE], F32)
+        z_odd = keep.tile([P, len(SHIFTS), len(SHIFTS), PAIR, SIDE, SIDE], F32)
         pv = keep.tile([P, len(SHIFTS), len(SHIFTS), PAIR, SIDE, SIDE], F32)
-        for planes in (z, pv):
+        for planes in (z_even, z_odd, pv):
             nc.vector.memset(planes[:, 0, :, :, 0, :], 0.0)
             nc.vector.memset(planes[:, 2, :, :, SIDE - 1, :], 0.0)
             nc.vector.memset(planes[:, :, 0, :, :, 0], 0.0)
@@ -182,7 +183,6 @@ def tile_merge_pa_kernel(
                     in_=y_bf[:, cols, :].rearrange("p x t -> p (x t)"),
                 )
 
-        z_planes = z[:].rearrange("p s t b i j -> p (s t) b (i j)")
         pv_blocks = pv[:].rearrange("p s t b (f i) j -> p (s t) (b f) (i j)", f=2)
         out_tiles = out.rearrange("b (r a) h w -> a r b (h w)", a=TILES)
 
@@ -218,6 +218,8 @@ def tile_merge_pa_kernel(
                 return total
 
             def window_attention(a, h, att, att_sum):
+                z = (z_even, z_odd)[h]
+                z_planes = z[:].rearrange("p s t b i j -> p (s t) b (i j)")
                 q_bank = project("q", a, h)
                 k_bank = project("k", a, h)
                 v_bank = project("v", a, h)
@@ -248,7 +250,7 @@ def tile_merge_pa_kernel(
 
                 e = work.tile([P, TAPS, PAIR, PIX], F32, tag="e")
                 for b in range(PAIR):
-                    nc.vector.tensor_tensor(
+                    nc.gpsimd.tensor_tensor(
                         out=e[:, :, b],
                         in0=z_planes[:, :, b],
                         in1=z_max[:, b].unsqueeze(1).to_broadcast([P, TAPS, PIX]),

@@ -18,6 +18,8 @@ PIX = SIDE * SIDE
 PAIR = 2
 CHUNK = PAIR * PIX
 TILES = CHANNELS // P
+HALVES = IMAGES // PAIR
+CHUNKS = TILES * HALVES
 SHIFTS = (-1, 0, 1)
 TAPS = len(SHIFTS) * len(SHIFTS)
 BLOCKS = CHUNK // P
@@ -62,6 +64,8 @@ def tile_merge_pa_kernel(
         gamma_pm = keep.tile([P, TILES, 2], F32)
         beta_pm = keep.tile([P, TILES, 2], F32)
         minus_slope = keep.tile([P, 1], F32)
+        minus_half = keep.tile([P, 1], F32)
+        nc.vector.memset(minus_half[:], -0.5)
         eps = keep.tile([P, 1], F32)
         nc.vector.memset(eps[:], BN_EPS)
 
@@ -175,7 +179,7 @@ def tile_merge_pa_kernel(
                     op0=ALU.mult,
                     op1=ALU.add,
                 )
-            for h in range(IMAGES // PAIR):
+            for h in range(HALVES):
                 cols = slice(h * CHUNK, (h + 1) * CHUNK)
                 nc.vector.quantize_mx(
                     out=y_codes[:, cols].bitcast(FP8X4),
@@ -183,13 +187,17 @@ def tile_merge_pa_kernel(
                     in_=y_bf[:, cols, :].rearrange("p x t -> p (x t)"),
                 )
 
+        z_pair = (z_even, z_odd)
         pv_blocks = pv[:].rearrange("p s t b (f i) j -> p (s t) (b f) (i j)", f=2)
         out_tiles = out.rearrange("b (r a) h w -> a r b (h w)", a=TILES)
+        q_of, k_of, v_of, e_of, den_of, num_of = {}, {}, {}, {}, {}, {}
+        r_den_of, att_of, sums_of, mean_of, var_of, r_std_of, above_of, below_of = {}, {}, {}, {}, {}, {}, {}, {}
 
-        with tc.tile_pool(name="work", bufs=2) as work, tc.psum_pool(name="banks", bufs=1) as banks:
+        with tc.tile_pool(name="work", bufs=2) as work, tc.psum_pool(name="banks", bufs=2) as banks, tc.manual_schedule():
 
-            def project(name, a, h):
-                bank = banks.tile([P, PAIR, SIDE, SIDE], F32, tag="bank_" + name)
+            def project(name, c, tag, bufs):
+                a, h = divmod(c, HALVES)
+                bank = banks.tile([P, PAIR, SIDE, SIDE], F32, tag=tag, bufs=bufs)
                 rows = slice(a * P, (a + 1) * P)
                 cols = slice(h * CHUNK, (h + 1) * CHUNK)
                 nc.tensor.matmul_mx(
@@ -202,6 +210,28 @@ def tile_merge_pa_kernel(
                     stop=True,
                 )
                 return bank
+
+            def project_qk(c):
+                q_bank = project("q", c, "short", 2)
+                k_of[c] = project("k", c, "bank_k", 1)
+                q_sb = work.tile([P, PAIR, SIDE, SIDE], F32, tag="q_sb")
+                nc.scalar.copy(out=q_sb[:], in_=q_bank[:])
+                q_of[c] = q_sb
+
+            def project_v(c):
+                v_of[c] = project("v", c, "bank_v", 1)
+
+            def times_neighbours(planes, bank, maps):
+                for s, di in enumerate(SHIFTS):
+                    i0, i1 = inside(di)
+                    for t, dj in enumerate(SHIFTS):
+                        j0, j1 = inside(dj)
+                        nc.vector.tensor_tensor(
+                            out=planes[:, s, t, :, i0:i1, j0:j1],
+                            in0=bank[:, :, i0 + di : i1 + di, j0 + dj : j1 + dj],
+                            in1=maps(s, t)[:, :, i0:i1, j0:j1],
+                            op=ALU.mult,
+                        )
 
             def sum_planes(blocks, tag):
                 total = banks.tile([P, BLOCKS, P], F32, tag=tag)
@@ -217,26 +247,11 @@ def tile_merge_pa_kernel(
                         )
                 return total
 
-            def window_attention(a, h, att, att_sum):
-                z = (z_even, z_odd)[h]
-                z_planes = z[:].rearrange("p s t b i j -> p (s t) b (i j)")
-                q_bank = project("q", a, h)
-                k_bank = project("k", a, h)
-                v_bank = project("v", a, h)
-                q_sb = work.tile([P, PAIR, SIDE, SIDE], F32, tag="q_sb")
-                nc.scalar.copy(out=q_sb[:], in_=q_bank[:])
+            def products(c):
+                times_neighbours(z_pair[c % 2], k_of[c], lambda s, t: q_of[c])
 
-                for s, di in enumerate(SHIFTS):
-                    i0, i1 = inside(di)
-                    for t, dj in enumerate(SHIFTS):
-                        j0, j1 = inside(dj)
-                        nc.vector.tensor_tensor(
-                            out=z[:, s, t, :, i0:i1, j0:j1],
-                            in0=k_bank[:, :, i0 + di : i1 + di, j0 + dj : j1 + dj],
-                            in1=q_sb[:, :, i0:i1, j0:j1],
-                            op=ALU.mult,
-                        )
-
+            def stabilise(c):
+                z_planes = z_pair[c % 2][:].rearrange("p s t b i j -> p (s t) b (i j)")
                 top = work.tile([P, 4, PAIR, PIX], F32, tag="top")
                 z_max = work.tile([P, PAIR, PIX], F32, tag="z_max")
                 for b in range(PAIR):
@@ -247,7 +262,6 @@ def tile_merge_pa_kernel(
                     nc.vector.tensor_max(out=top[:, 0, b], in0=top[:, 0, b], in1=top[:, 1, b])
                 for b in range(PAIR):
                     nc.vector.tensor_max(out=z_max[:, b], in0=top[:, 0, b], in1=z_planes[:, 8, b])
-
                 e = work.tile([P, TAPS, PAIR, PIX], F32, tag="e")
                 for b in range(PAIR):
                     nc.gpsimd.tensor_tensor(
@@ -257,73 +271,134 @@ def tile_merge_pa_kernel(
                         op=ALU.subtract,
                     )
                     nc.scalar.activation(out=e[:, :, b], in_=e[:, :, b], func=ACT.Exp)
+                e_of[c] = e
 
-                den_t = sum_planes(e[:].rearrange("p d b (f x) -> p d (b f) x", f=2), "den_t")
-                ln_den = work.tile([P, BLOCKS, P], F32, tag="ln_den")
-                nc.scalar.activation(out=ln_den[:], in_=den_t[:], func=ACT.Ln)
-                r_den = work.tile([P, BLOCKS, P], F32, tag="r_den")
+            def sum_e(c):
+                den_of[c] = sum_planes(e_of[c][:].rearrange("p d b (f x) -> p d (b f) x", f=2), "den_t")
+
+            def weigh(c):
+                e_maps = e_of[c][:].rearrange("p (s t) b (i j) -> p s t b i j", s=len(SHIFTS), i=SIDE)
+                times_neighbours(pv, v_of[c], lambda s, t: e_maps[:, s, t])
+                num_of[c] = sum_planes(pv_blocks, "num_t")
+
+            def reciprocal(a):
+                ln_den = work.tile([P, HALVES, BLOCKS, P], F32, tag="ln_den", bufs=1)
+                for h in range(HALVES):
+                    nc.scalar.activation(out=ln_den[:, h], in_=den_of[a * HALVES + h][:], func=ACT.Ln)
+                r_den = work.tile([P, HALVES, BLOCKS, P], F32, tag="r_den")
                 nc.scalar.activation(out=r_den[:], in_=ln_den[:], func=ACT.Exp, scale=-1.0)
+                r_den_of[a] = r_den
 
-                e_maps = e[:].rearrange("p (s t) b (i j) -> p s t b i j", s=len(SHIFTS), i=SIDE)
-                for s, di in enumerate(SHIFTS):
-                    i0, i1 = inside(di)
-                    for t, dj in enumerate(SHIFTS):
-                        j0, j1 = inside(dj)
-                        nc.vector.tensor_tensor(
-                            out=pv[:, s, t, :, i0:i1, j0:j1],
-                            in0=v_bank[:, :, i0 + di : i1 + di, j0 + dj : j1 + dj],
-                            in1=e_maps[:, s, t, :, i0:i1, j0:j1],
-                            op=ALU.mult,
-                        )
-                num_t = sum_planes(pv_blocks, "num_t")
+            def divide(a):
+                att = work.tile([P, HALVES, CHUNK], F32, tag="att")
+                att_sums = work.tile([P, HALVES], F32, tag="att_sums")
+                for h in range(HALVES):
+                    att_t = work.tile([P, BLOCKS, P], F32, tag="att_t")
+                    nc.vector.tensor_mul(out=att_t[:], in0=num_of[a * HALVES + h][:], in1=r_den_of[a][:, h])
+                    att_bank = banks.tile([P, BLOCKS, P], F32, tag="short")
+                    for g in range(BLOCKS):
+                        nc.tensor.transpose(att_bank[:, g, :], att_t[:, g, :], ident[:])
+                    nc.scalar.activation(
+                        out=att[:, h, :],
+                        in_=att_bank[:].rearrange("p g x -> p (g x)"),
+                        func=ACT.Copy,
+                        accum_out=att_sums[:, h : h + 1],
+                    )
+                att_of[a], sums_of[a] = att, att_sums
 
-                att_t = work.tile([P, BLOCKS, P], F32, tag="att_t")
-                nc.vector.tensor_mul(out=att_t[:], in0=num_t[:], in1=r_den[:])
-                att_bank = banks.tile([P, BLOCKS, P], F32, tag="att_bank")
-                for g in range(BLOCKS):
-                    nc.tensor.transpose(att_bank[:, g, :], att_t[:, g, :], ident[:])
-                nc.scalar.activation(
-                    out=att, in_=att_bank[:].rearrange("p g x -> p (g x)"), func=ACT.Copy, accum_out=att_sum
-                )
-
-            for a in range(TILES):
-                att = work.tile([P, IMAGES * PIX], F32, tag="att")
-                att_sums = work.tile([P, IMAGES // PAIR], F32, tag="att_sums")
-                for h in range(IMAGES // PAIR):
-                    window_attention(a, h, att[:, h * CHUNK : (h + 1) * CHUNK], att_sums[:, h : h + 1])
-
+            def statistics(a):
+                parts = work.tile([P, HALVES], F32, tag="parts")
+                nc.scalar.activation(out=parts[:], in_=sums_of[a][:], func=ACT.Copy, scale=-1.0 / BN_COUNT)
                 minus_mean = work.tile([P, 1], F32, tag="minus_mean")
-                nc.vector.tensor_scalar(
-                    out=minus_mean[:],
-                    in0=att_sums[:, 0:1],
-                    scalar1=att_sums[:, 1:2],
-                    scalar2=-1.0 / BN_COUNT,
-                    op0=ALU.add,
-                    op1=ALU.mult,
-                )
-                squares = work.tile([P, IMAGES * PIX], F32, tag="squares")
+                nc.scalar.activation(out=minus_mean[:], in_=parts[:, 0:1], func=ACT.Identity, bias=parts[:, 1:2])
+                squares = work.tile([P, HALVES * CHUNK], F32, tag="squares", bufs=1)
                 sum_squares = work.tile([P, 1], F32, tag="sum_squares")
                 nc.scalar.activation(
-                    out=squares[:], in_=att[:], func=ACT.Square, bias=minus_mean[:], accum_out=sum_squares[:]
+                    out=squares[:],
+                    in_=att_of[a][:].rearrange("p h x -> p (h x)"),
+                    func=ACT.Square,
+                    bias=minus_mean[:],
+                    accum_out=sum_squares[:],
                 )
-                ln_var = work.tile([P, 1], F32, tag="ln_var")
+                var_eps = work.tile([P, 1], F32, tag="var_eps")
                 nc.scalar.activation(
-                    out=ln_var[:], in_=sum_squares[:], func=ACT.Ln, scale=1.0 / BN_COUNT, bias=eps[:]
+                    out=var_eps[:], in_=sum_squares[:], func=ACT.Identity, scale=1.0 / BN_COUNT, bias=eps[:]
                 )
+                mean_of[a], var_of[a] = minus_mean, var_eps
+
+            def rsqrt(a):
                 r_std = work.tile([P, 1], F32, tag="r_std")
-                nc.scalar.activation(out=r_std[:], in_=ln_var[:], func=ACT.Exp, scale=-0.5)
+                nc.gpsimd.tensor_tensor(out=r_std[:], in0=var_of[a][:], in1=minus_half[:], op=ALU.pow)
+                r_std_of[a] = r_std
+
+            def affine(a):
                 gain = work.tile([P, 2], F32, tag="gain")
-                nc.vector.tensor_scalar_mul(out=gain[:], in0=gamma_pm[:, a, :], scalar1=r_std[:])
+                nc.scalar.activation(out=gain[:], in_=gamma_pm[:, a, :], func=ACT.Copy, scale=r_std_of[a][:])
                 shift = work.tile([P, 2], F32, tag="shift")
-                nc.vector.scalar_tensor_tensor(
-                    out=shift[:], in0=gain[:], scalar=minus_mean[:], in1=beta_pm[:, a, :], op0=ALU.mult, op1=ALU.add
-                )
-                above = work.tile([P, IMAGES * PIX], F32, tag="above")
-                nc.scalar.activation(out=above[:], in_=att[:], func=ACT.Relu, scale=gain[:, 0:1], bias=shift[:, 0:1])
-                below = work.tile([P, IMAGES * PIX], F32, tag="below")
-                nc.scalar.activation(out=below[:], in_=att[:], func=ACT.Relu, scale=gain[:, 1:2], bias=shift[:, 1:2])
-                result = work.tile([P, IMAGES * PIX], F32, tag="result")
-                nc.vector.scalar_tensor_tensor(
-                    out=result[:], in0=below[:], scalar=minus_slope[:], in1=above[:], op0=ALU.mult, op1=ALU.add
-                )
-                nc.sync.dma_start(out=out_tiles[a], in_=result[:].rearrange("p (b x) -> p b x", b=IMAGES))
+                for sign in range(2):
+                    nc.scalar.activation(
+                        out=shift[:, sign : sign + 1],
+                        in_=gain[:, sign : sign + 1],
+                        func=ACT.Identity,
+                        scale=mean_of[a][:],
+                        bias=beta_pm[:, a, sign : sign + 1],
+                    )
+                above = work.tile([P, HALVES, CHUNK], F32, tag="above")
+                below = work.tile([P, HALVES, CHUNK], F32, tag="below")
+                for h in range(HALVES):
+                    nc.scalar.activation(
+                        out=above[:, h], in_=att_of[a][:, h], func=ACT.Relu, scale=gain[:, 0:1], bias=shift[:, 0:1]
+                    )
+                    nc.scalar.activation(
+                        out=below[:, h], in_=att_of[a][:, h], func=ACT.Relu, scale=gain[:, 1:2], bias=shift[:, 1:2]
+                    )
+                above_of[a], below_of[a] = above, below
+
+            def finish(a):
+                result = work.tile([P, HALVES, CHUNK], F32, tag="result")
+                for h in range(HALVES):
+                    nc.vector.scalar_tensor_tensor(
+                        out=result[:, h],
+                        in0=below_of[a][:, h],
+                        scalar=minus_slope[:],
+                        in1=above_of[a][:, h],
+                        op0=ALU.mult,
+                        op1=ALU.add,
+                    )
+                    nc.sync.dma_start(
+                        out=out_tiles[a][:, h * PAIR : (h + 1) * PAIR, :],
+                        in_=result[:, h].rearrange("p (b x) -> p b x", b=PAIR),
+                    )
+
+            def live(c):
+                return 0 <= c < CHUNKS
+
+            def group_due(r, lag):
+                a, rest = divmod(r - lag, HALVES)
+                return a if rest == 0 and 0 <= a < TILES else None
+
+            project_qk(0)
+            for r in range(CHUNKS + 4):
+                if live(r):
+                    products(r)
+                if live(r + 1):
+                    project_qk(r + 1)
+                if group_due(r, 3) is not None:
+                    divide(group_due(r, 3))
+                    statistics(group_due(r, 3))
+                if live(r - 1):
+                    sum_e(r - 1)
+                if group_due(r, 4) is not None:
+                    affine(group_due(r, 4))
+                if group_due(r, 2) is not None:
+                    reciprocal(group_due(r, 2))
+                if group_due(r, 5) is not None:
+                    finish(group_due(r, 5))
+                if live(r):
+                    stabilise(r)
+                if live(r - 1):
+                    weigh(r - 1)
+                if live(r):
+                    project_v(r)
+                if group_due(r, 3) is not None:
+                    rsqrt(group_due(r, 3))

@@ -39,10 +39,7 @@ def tile_merge_pa_kernel(
     nc = tc.nc
     weights = {"c1": w_c1, "q": w_q, "k": w_k, "v": w_v}
 
-    with tc.tile_pool(name="keep", bufs=1) as keep:
-        ident = keep.tile([P, P], F32)
-        make_identity(nc, ident[:])
-
+    with tc.tile_pool(name="keep", bufs=1) as keep, tc.psum_pool(name="banks", bufs=2) as banks, tc.manual_schedule():
         w_codes = {}
         w_scales = {}
         for name in weights:
@@ -50,35 +47,27 @@ def tile_merge_pa_kernel(
             w_scales[name] = keep.tile([P, CHANNELS], U8, name="scales_" + name, align_bytes=64)
         y_codes = keep.tile([P, IMAGES * PIX], U32, align_bytes=64)
         y_scales = keep.tile([P, IMAGES * PIX], U8, align_bytes=64)
-
-        z_even = keep.tile([P, len(SHIFTS), len(SHIFTS), PAIR, SIDE, SIDE], F32)
-        z_odd = keep.tile([P, len(SHIFTS), len(SHIFTS), PAIR, SIDE, SIDE], F32)
-        pv = keep.tile([P, len(SHIFTS), len(SHIFTS), PAIR, SIDE, SIDE], F32)
-        for planes in (z_even, z_odd, pv):
-            nc.vector.memset(planes[:, 0, :, :, 0, :], 0.0)
-            nc.vector.memset(planes[:, 2, :, :, SIDE - 1, :], 0.0)
-            nc.vector.memset(planes[:, :, 0, :, :, 0], 0.0)
-            nc.vector.memset(planes[:, :, 2, :, :, SIDE - 1], 0.0)
-
         bias_c1 = keep.tile([P, PACK], F32)
         gamma_pm = keep.tile([P, TILES, 2], F32)
         beta_pm = keep.tile([P, TILES, 2], F32)
         minus_slope = keep.tile([P, 1], F32)
         minus_half = keep.tile([P, 1], F32)
-        nc.vector.memset(minus_half[:], -0.5)
         eps = keep.tile([P, 1], F32)
-        nc.vector.memset(eps[:], BN_EPS)
+        ident = keep.tile([P, P], F32)
+        z_even = keep.tile([P, len(SHIFTS), len(SHIFTS), PAIR, SIDE, SIDE], F32)
+        z_odd = keep.tile([P, len(SHIFTS), len(SHIFTS), PAIR, SIDE, SIDE], F32)
+        pv = keep.tile([P, len(SHIFTS), len(SHIFTS), PAIR, SIDE, SIDE], F32)
 
-        with tc.tile_pool(name="head", bufs=2) as head, tc.psum_pool(name="head_banks", bufs=4) as head_banks:
+        with tc.tile_pool(name="head", bufs=2) as head:
             x_sb = []
             w_raw = {}
 
             def load_image(b):
-                x_sb.append(head.tile([P, PACK * 4 * PIX], BF16, name="x%d" % b, bufs=1))
-                nc.sync.dma_start(
-                    out=x_sb[b][:].rearrange("p (u f) -> p u f", u=2),
-                    in_=x[b].rearrange("(u p e) h w -> p u (e h w)", u=2, e=2),
-                )
+                x_sb.append(head.tile([P, 2, 2 * 4 * PIX], BF16, name="x%d" % b, bufs=1))
+                for u in range(2):
+                    nc.sync.dma_start(
+                        out=x_sb[b][:, u, :], in_=x[b].rearrange("(u p e) h w -> u p (e h w)", u=2, e=2)[u]
+                    )
 
             def load_weight(name, runs, rows):
                 w_raw[name] = head.tile([P, TILES * CHANNELS], BF16, name="raw_" + name, bufs=1)
@@ -103,19 +92,29 @@ def tile_merge_pa_kernel(
             slope_bf = head.tile([P, 1], BF16, bufs=1)
             nc.scalar.dma_start(out=slope_bf[:], in_=prelu_a.partition_broadcast(P))
 
-            nc.vector.tensor_copy(out=bias_c1[:], in_=b1_bf[:])
-            nc.vector.tensor_copy(out=gamma_pm[:, :, 0], in_=gamma_bf[:])
-            nc.vector.tensor_scalar_mul(out=gamma_pm[:, :, 1], in0=gamma_bf[:], scalar1=-1.0)
-            nc.vector.tensor_copy(out=beta_pm[:, :, 0], in_=beta_bf[:])
-            nc.vector.tensor_scalar_mul(out=beta_pm[:, :, 1], in0=beta_bf[:], scalar1=-1.0)
-            nc.vector.tensor_scalar_mul(out=minus_slope[:], in0=slope_bf[:], scalar1=-1.0)
+            make_identity(nc, ident[:])
+            for planes in (z_even, z_odd, pv):
+                nc.vector.memset(planes[:, 0, :, :, 0, :], 0.0)
+                nc.vector.memset(planes[:, 2, :, :, SIDE - 1, :], 0.0)
+                nc.vector.memset(planes[:, :, 0, :, :, 0], 0.0)
+                nc.vector.memset(planes[:, :, 2, :, :, SIDE - 1], 0.0)
+            nc.vector.memset(minus_half[:], -0.5)
+            nc.vector.memset(eps[:], BN_EPS)
+            nc.scalar.copy(out=bias_c1[:], in_=b1_bf[:])
+            nc.scalar.copy(out=gamma_pm[:, :, 0], in_=gamma_bf[:])
+            nc.scalar.mul(out=gamma_pm[:, :, 1], in_=gamma_bf[:], mul=-1.0)
+            nc.scalar.copy(out=beta_pm[:, :, 0], in_=beta_bf[:])
+            nc.scalar.mul(out=beta_pm[:, :, 1], in_=beta_bf[:], mul=-1.0)
+            nc.scalar.mul(out=minus_slope[:], in_=slope_bf[:], mul=-1.0)
 
-            def quantise_weight(name):
+            grouped_of = {}
+
+            def turn_weight(name):
                 words = w_raw[name][:].bitcast(F32)
-                grouped = head.tile([P, TILES * P * PACK], BF16, tag="grouped", align_bytes=64)
+                grouped = head.tile([P, TILES * P * PACK], BF16, tag="grouped", bufs=len(weights), align_bytes=64)
                 grouped_words = grouped[:].bitcast(F32).rearrange("p (a r u) -> p a r u", a=TILES, u=2)
                 for first in range(0, TILES, 2):
-                    turned = head_banks.tile([P, 2, 2, P], F32, tag="turned")
+                    turned = banks.tile([P, 2, 2, P], F32, tag="den_t")
                     for a in range(2):
                         for u in range(2):
                             col = ((first + a) * 2 + u) * P
@@ -124,46 +123,56 @@ def tile_merge_pa_kernel(
                         out=grouped_words[:, first : first + 2],
                         in_=turned[:].rearrange("p a u r -> p a r u"),
                     )
-                nc.vector.quantize_mx(
-                    out=w_codes[name][:].bitcast(FP8X4), scales=w_scales[name][:], in_=grouped[:]
-                )
+                grouped_of[name] = grouped
 
-            quantise_weight("c1")
+            def quantise_weight(name):
+                nc.vector.quantize_mx(
+                    out=w_codes[name][:].bitcast(FP8X4), scales=w_scales[name][:], in_=grouped_of[name][:]
+                )
 
             ll_codes = head.tile([P, IMAGES * PIX], U32, bufs=1, align_bytes=64)
             ll_scales = head.tile([P, IMAGES * PIX], U8, bufs=1, align_bytes=64)
-            for b in range(IMAGES):
-                row_pairs = x_sb[b][:].rearrange("p (r two w) -> p r two w", two=2, w=2 * SIDE)
+            row_sums_of = {}
+            ll2_of = {}
+
+            def add_rows(b):
+                row_pairs = x_sb[b][:].rearrange("p u (r two w) -> p u r two w", two=2, w=2 * SIDE)
                 row_sums = head.tile([P, PACK * PIX * 2], F32, tag="row_sums")
-                nc.vector.tensor_tensor(
-                    out=row_sums[:].rearrange("p (r w) -> p r w", w=2 * SIDE),
-                    in0=row_pairs[:, :, 0, :],
-                    in1=row_pairs[:, :, 1, :],
-                    op=ALU.add,
-                )
-                col_pairs = row_sums[:].rearrange("p (t x two) -> p x t two", t=PACK, two=2)
+                for u in range(2):
+                    nc.vector.tensor_tensor(
+                        out=row_sums[:].rearrange("p (u r w) -> p u r w", u=2, w=2 * SIDE)[:, u],
+                        in0=row_pairs[:, u, :, 0, :],
+                        in1=row_pairs[:, u, :, 1, :],
+                        op=ALU.add,
+                    )
+                row_sums_of[b] = row_sums
+
+            def add_columns(b):
+                col_pairs = row_sums_of[b][:].rearrange("p (t x two) -> p x t two", t=PACK, two=2)
                 ll2 = head.tile([P, PIX, PACK], BF16, tag="ll2", align_bytes=64)
                 nc.vector.tensor_tensor(
                     out=ll2[:], in0=col_pairs[:, :, :, 0], in1=col_pairs[:, :, :, 1], op=ALU.add
                 )
+                ll2_of[b] = ll2
+
+            def quantise_ll(b):
                 cols = slice(b * PIX, (b + 1) * PIX)
                 nc.vector.quantize_mx(
                     out=ll_codes[:, cols].bitcast(FP8X4),
                     scales=ll_scales[:, cols],
-                    in_=ll2[:].rearrange("p x t -> p (x t)"),
+                    in_=ll2_of[b][:].rearrange("p x t -> p (x t)"),
                 )
 
-            for name in ("q", "k", "v"):
-                quantise_weight(name)
-
+            y_rows = head.tile([P, PACK, IMAGES * PIX], BF16, bufs=1)
             y_bf = head.tile([P, IMAGES * PIX, PACK], BF16, bufs=1, align_bytes=64)
-            for g in range(IMAGES * PIX // P):
-                cols = slice(g * P, (g + 1) * P)
-                y_bank = head_banks.tile([P, PACK, P], F32, tag="y_bank")
+
+            def first_convolution(h):
+                cols = slice(h * CHUNK, (h + 1) * CHUNK)
                 for t in range(PACK):
                     rows = slice(t * P, (t + 1) * P)
+                    y_bank = banks.tile([P, CHUNK], F32, tag="num_t")
                     nc.tensor.matmul_mx(
-                        out=y_bank[:, t, :],
+                        out=y_bank[:],
                         lhsT=w_codes["c1"][:, rows].bitcast(FP8X4),
                         lhsT_scale=w_scales["c1"][:, rows],
                         rhs=ll_codes[:, cols].bitcast(FP8X4),
@@ -171,15 +180,15 @@ def tile_merge_pa_kernel(
                         start=True,
                         stop=True,
                     )
-                nc.vector.scalar_tensor_tensor(
-                    out=y_bf[:, cols, :],
-                    in0=y_bank[:].rearrange("p t x -> p x t"),
-                    scalar=0.5,
-                    in1=bias_c1[:].unsqueeze(1).to_broadcast([P, P, PACK]),
-                    op0=ALU.mult,
-                    op1=ALU.add,
-                )
-            for h in range(HALVES):
+                    nc.scalar.activation(
+                        out=y_rows[:, t, cols], in_=y_bank[:], func=ACT.Identity, scale=0.5, bias=bias_c1[:, t : t + 1]
+                    )
+
+            def group_y(h):
+                cols = slice(h * CHUNK, (h + 1) * CHUNK)
+                nc.vector.tensor_copy(out=y_bf[:, cols, :], in_=y_rows[:, :, cols].rearrange("p t x -> p x t"))
+
+            def quantise_y(h):
                 cols = slice(h * CHUNK, (h + 1) * CHUNK)
                 nc.vector.quantize_mx(
                     out=y_codes[:, cols].bitcast(FP8X4),
@@ -187,13 +196,40 @@ def tile_merge_pa_kernel(
                     in_=y_bf[:, cols, :].rearrange("p x t -> p (x t)"),
                 )
 
+            turn_weight("c1")
+            add_rows(0)
+            add_columns(0)
+            add_rows(1)
+            quantise_ll(0)
+            quantise_weight("c1")
+            add_columns(1)
+            add_rows(2)
+            quantise_ll(1)
+            turn_weight("q")
+            first_convolution(0)
+            turn_weight("k")
+            turn_weight("v")
+            add_columns(2)
+            add_rows(3)
+            quantise_ll(2)
+            add_columns(3)
+            quantise_weight("q")
+            quantise_ll(3)
+            first_convolution(1)
+            group_y(0)
+            quantise_weight("k")
+            quantise_y(0)
+            quantise_weight("v")
+            group_y(1)
+            quantise_y(1)
+
         z_pair = (z_even, z_odd)
         pv_blocks = pv[:].rearrange("p s t b (f i) j -> p (s t) (b f) (i j)", f=2)
         out_tiles = out.rearrange("b (r a) h w -> a r b (h w)", a=TILES)
         q_of, k_of, v_of, e_of, den_of, num_of = {}, {}, {}, {}, {}, {}
         r_den_of, att_of, sums_of, mean_of, var_of, r_std_of, above_of, below_of = {}, {}, {}, {}, {}, {}, {}, {}
 
-        with tc.tile_pool(name="work", bufs=2) as work, tc.psum_pool(name="banks", bufs=2) as banks, tc.manual_schedule():
+        with tc.tile_pool(name="work", bufs=2) as work:
 
             def project(name, c, tag, bufs):
                 a, h = divmod(c, HALVES)
@@ -264,7 +300,9 @@ def tile_merge_pa_kernel(
                     nc.vector.tensor_max(out=z_max[:, b], in0=top[:, 0, b], in1=z_planes[:, 8, b])
                 e = work.tile([P, TAPS, PAIR, PIX], F32, tag="e")
                 for b in range(PAIR):
-                    nc.gpsimd.tensor_tensor(
+                    idle_vector = c == CHUNKS - 1 or (c == 0 and b == PAIR - 1)
+                    subtractor = nc.vector if idle_vector else nc.gpsimd
+                    subtractor.tensor_tensor(
                         out=e[:, :, b],
                         in0=z_planes[:, :, b],
                         in1=z_max[:, b].unsqueeze(1).to_broadcast([P, TAPS, PIX]),

@@ -51,6 +51,10 @@ def tile_merge_pa_kernel(
         gamma_pm = keep.tile([P, TILES, 2], F32)
         beta_pm = keep.tile([P, TILES, 2], F32)
         minus_slope = keep.tile([P, 1], F32)
+        b1_bf = keep.tile([P, PACK], BF16)
+        gamma_bf = keep.tile([P, TILES], BF16)
+        beta_bf = keep.tile([P, TILES], BF16)
+        slope_bf = keep.tile([P, 1], BF16)
         minus_half = keep.tile([P, 1], F32)
         eps = keep.tile([P, 1], F32)
         ident = keep.tile([P, P], F32)
@@ -75,22 +79,17 @@ def tile_merge_pa_kernel(
 
             load_image(0)
             load_weight("c1", 2, w_c1.rearrange("(u r e) c -> r u (e c)", u=2, e=2))
+            nc.sync.dma_start(
+                out=b1_bf[:].rearrange("r (u e) -> r u e", u=2),
+                in_=b_c1.rearrange("(u r e) -> r u e", u=2, e=2),
+            )
             for b in range(1, IMAGES):
                 load_image(b)
             for name in ("q", "k", "v"):
                 load_weight(name, 1, weights[name].rearrange("(r u a) m -> r u (a m)", u=1, a=TILES))
-
-            b1_bf = head.tile([P, PACK], BF16, bufs=1)
-            nc.scalar.dma_start(
-                out=b1_bf[:].rearrange("r (u e) -> r u e", u=2),
-                in_=b_c1.rearrange("(u r e) -> r u e", u=2, e=2),
-            )
-            gamma_bf = head.tile([P, TILES], BF16, bufs=1)
-            nc.scalar.dma_start(out=gamma_bf[:], in_=bn_gamma.rearrange("(r a) -> r a", a=TILES))
-            beta_bf = head.tile([P, TILES], BF16, bufs=1)
-            nc.scalar.dma_start(out=beta_bf[:], in_=bn_beta.rearrange("(r a) -> r a", a=TILES))
-            slope_bf = head.tile([P, 1], BF16, bufs=1)
-            nc.scalar.dma_start(out=slope_bf[:], in_=prelu_a.partition_broadcast(P))
+            nc.sync.dma_start(out=gamma_bf[:], in_=bn_gamma.rearrange("(r a) -> r a", a=TILES))
+            nc.sync.dma_start(out=beta_bf[:], in_=bn_beta.rearrange("(r a) -> r a", a=TILES))
+            nc.sync.dma_start(out=slope_bf[:], in_=prelu_a.partition_broadcast(P))
 
             make_identity(nc, ident[:])
             for planes in (z_even, z_odd, pv):
@@ -100,12 +99,6 @@ def tile_merge_pa_kernel(
                 nc.vector.memset(planes[:, :, 2, :, :, SIDE - 1], 0.0)
             nc.vector.memset(minus_half[:], -0.5)
             nc.vector.memset(eps[:], BN_EPS)
-            nc.scalar.copy(out=bias_c1[:], in_=b1_bf[:])
-            nc.scalar.copy(out=gamma_pm[:, :, 0], in_=gamma_bf[:])
-            nc.scalar.mul(out=gamma_pm[:, :, 1], in_=gamma_bf[:], mul=-1.0)
-            nc.scalar.copy(out=beta_pm[:, :, 0], in_=beta_bf[:])
-            nc.scalar.mul(out=beta_pm[:, :, 1], in_=beta_bf[:], mul=-1.0)
-            nc.scalar.mul(out=minus_slope[:], in_=slope_bf[:], mul=-1.0)
 
             grouped_of = {}
 
@@ -197,6 +190,7 @@ def tile_merge_pa_kernel(
                 )
 
             turn_weight("c1")
+            nc.scalar.copy(out=bias_c1[:], in_=b1_bf[:])
             add_rows(0)
             add_columns(0)
             add_rows(1)
@@ -416,6 +410,11 @@ def tile_merge_pa_kernel(
                 return a if rest == 0 and 0 <= a < TILES else None
 
             project_qk(0)
+            nc.scalar.copy(out=gamma_pm[:, :, 0], in_=gamma_bf[:])
+            nc.scalar.mul(out=gamma_pm[:, :, 1], in_=gamma_bf[:], mul=-1.0)
+            nc.scalar.copy(out=beta_pm[:, :, 0], in_=beta_bf[:])
+            nc.scalar.mul(out=beta_pm[:, :, 1], in_=beta_bf[:], mul=-1.0)
+            nc.scalar.mul(out=minus_slope[:], in_=slope_bf[:], mul=-1.0)
             for r in range(CHUNKS + 4):
                 if live(r):
                     products(r)

import concourse.mybir as mybir
from concourse.masks import make_identity

F32 = mybir.dt.float32
BF16 = mybir.dt.bfloat16
U32 = mybir.dt.uint32
U8 = mybir.dt.uint8
FP8X4 = mybir.dt.float8_e4m3fn_x4
ALU = mybir.AluOpType
ACT = mybir.ActivationFunctionType

P = 128
PACK = 4
IMAGES = 4
CHANNELS = 512
SIDE = 16
PIX = SIDE * SIDE
PAIR = 2
CHUNK = PAIR * PIX
TILES = CHANNELS // P
HALVES = IMAGES // PAIR
CHUNKS = TILES * HALVES
SHIFTS = (-1, 0, 1)
TAPS = len(SHIFTS) * len(SHIFTS)
BLOCKS = CHUNK // P
BN_EPS = 1e-5
BN_COUNT = IMAGES * PIX

FLOPS = 4 * 2 * CHANNELS * CHANNELS * IMAGES * PIX


def inside(shift):
    return max(0, -shift), SIDE - max(0, shift)


def tile_merge_pa_kernel(
    tc, x, w_c1, b_c1, w_q, w_k, w_v, bn_gamma, bn_beta, prelu_a, out
):
    nc = tc.nc
    weights = {"c1": w_c1, "q": w_q, "k": w_k, "v": w_v}

    with tc.tile_pool(name="keep", bufs=1) as keep, tc.psum_pool(name="banks", bufs=2) as banks, tc.manual_schedule():
        w_codes = {}
        w_scales = {}
        for name in weights:
            w_codes[name] = keep.tile([P, CHANNELS], U32, name="codes_" + name, align_bytes=64)
            w_scales[name] = keep.tile([P, CHANNELS], U8, name="scales_" + name, align_bytes=64)
        y_codes = keep.tile([P, IMAGES * PIX], U32, align_bytes=64)
        y_scales = keep.tile([P, IMAGES * PIX], U8, align_bytes=64)
        bias_c1 = keep.tile([P, PACK], F32)
        gamma_pm = keep.tile([P, TILES, 2], F32)
        beta_pm = keep.tile([P, TILES, 2], F32)
        minus_slope = keep.tile([P, 1], F32)
        b1_bf = keep.tile([P, PACK], BF16)
        gamma_bf = keep.tile([P, TILES], BF16)
        beta_bf = keep.tile([P, TILES], BF16)
        slope_bf = keep.tile([P, 1], BF16)
        minus_half = keep.tile([P, 1], F32)
        eps = keep.tile([P, 1], F32)
        ident = keep.tile([P, P], F32)
        z_even = keep.tile([P, len(SHIFTS), len(SHIFTS), PAIR, SIDE, SIDE], F32)
        z_odd = keep.tile([P, len(SHIFTS), len(SHIFTS), PAIR, SIDE, SIDE], F32)
        pv = keep.tile([P, len(SHIFTS), len(SHIFTS), PAIR, SIDE, SIDE], F32)

        with tc.tile_pool(name="head", bufs=2) as head:
            x_sb = []
            w_raw = {}

            def load_image(b):
                x_sb.append(head.tile([P, 2, 2 * 4 * PIX], BF16, name="x%d" % b, bufs=1))
                for u in range(2):
                    nc.sync.dma_start(
                        out=x_sb[b][:, u, :], in_=x[b].rearrange("(u p e) h w -> u p (e h w)", u=2, e=2)[u]
                    )

            def load_weight(name, runs, rows):
                w_raw[name] = head.tile([P, TILES * CHANNELS], BF16, name="raw_" + name, bufs=1)
                nc.sync.dma_start(out=w_raw[name][:].rearrange("r (u f) -> r u f", u=runs), in_=rows)

            load_image(0)
            load_weight("c1", 2, w_c1.rearrange("(u r e) c -> r u (e c)", u=2, e=2))
            nc.sync.dma_start(
                out=b1_bf[:].rearrange("r (u e) -> r u e", u=2),
                in_=b_c1.rearrange("(u r e) -> r u e", u=2, e=2),
            )
            for b in range(1, IMAGES):
                load_image(b)
            for name in ("q", "k", "v"):
                load_weight(name, 1, weights[name].rearrange("(r u a) m -> r u (a m)", u=1, a=TILES))
            nc.sync.dma_start(out=gamma_bf[:], in_=bn_gamma.rearrange("(r a) -> r a", a=TILES))
            nc.sync.dma_start(out=beta_bf[:], in_=bn_beta.rearrange("(r a) -> r a", a=TILES))
            nc.sync.dma_start(out=slope_bf[:], in_=prelu_a.partition_broadcast(P))

            make_identity(nc, ident[:])
            for planes in (z_even, z_odd, pv):
                nc.vector.memset(planes[:, 0, :, :, 0, :], 0.0)
                nc.vector.memset(planes[:, 2, :, :, SIDE - 1, :], 0.0)
                nc.vector.memset(planes[:, :, 0, :, :, 0], 0.0)
                nc.vector.memset(planes[:, :, 2, :, :, SIDE - 1], 0.0)
            nc.vector.memset(minus_half[:], -0.5)
            nc.vector.memset(eps[:], BN_EPS)

            grouped_of = {}

            def turn_weight(name):
                words = w_raw[name][:].bitcast(F32)
                grouped = head.tile([P, TILES * P * PACK], BF16, tag="grouped", bufs=len(weights), align_bytes=64)
                grouped_words = grouped[:].bitcast(F32).rearrange("p (a r u) -> p a r u", a=TILES, u=2)
                for first in range(0, TILES, 2):
                    turned = banks.tile([P, 2, 2, P], F32, tag="den_t")
                    for a in range(2):
                        for u in range(2):
                            col = ((first + a) * 2 + u) * P
                            nc.tensor.transpose(turned[:, a, u, :], words[:, col : col + P], ident[:])
                    nc.scalar.copy(
                        out=grouped_words[:, first : first + 2],
                        in_=turned[:].rearrange("p a u r -> p a r u"),
                    )
                grouped_of[name] = grouped

            def quantise_weight(name):
                nc.vector.quantize_mx(
                    out=w_codes[name][:].bitcast(FP8X4), scales=w_scales[name][:], in_=grouped_of[name][:]
                )

            ll_codes = head.tile([P, IMAGES * PIX], U32, bufs=1, align_bytes=64)
            ll_scales = head.tile([P, IMAGES * PIX], U8, bufs=1, align_bytes=64)
            row_sums_of = {}
            ll2_of = {}

            def add_rows(b):
                row_pairs = x_sb[b][:].rearrange("p u (r two w) -> p u r two w", two=2, w=2 * SIDE)
                row_sums = head.tile([P, PACK * PIX * 2], F32, tag="row_sums")
                for u in range(2):
                    nc.vector.tensor_tensor(
                        out=row_sums[:].rearrange("p (u r w) -> p u r w", u=2, w=2 * SIDE)[:, u],
                        in0=row_pairs[:, u, :, 0, :],
                        in1=row_pairs[:, u, :, 1, :],
                        op=ALU.add,
                    )
                row_sums_of[b] = row_sums

            def add_columns(b):
                col_pairs = row_sums_of[b][:].rearrange("p (t x two) -> p x t two", t=PACK, two=2)
                ll2 = head.tile([P, PIX, PACK], BF16, tag="ll2", align_bytes=64)
                nc.vector.tensor_tensor(
                    out=ll2[:], in0=col_pairs[:, :, :, 0], in1=col_pairs[:, :, :, 1], op=ALU.add
                )
                ll2_of[b] = ll2

            def quantise_ll(b):
                cols = slice(b * PIX, (b + 1) * PIX)
                nc.vector.quantize_mx(
                    out=ll_codes[:, cols].bitcast(FP8X4),
                    scales=ll_scales[:, cols],
                    in_=ll2_of[b][:].rearrange("p x t -> p (x t)"),
                )

            y_rows = head.tile([P, PACK, IMAGES * PIX], BF16, bufs=1)
            y_bf = head.tile([P, IMAGES * PIX, PACK], BF16, bufs=1, align_bytes=64)

            def first_convolution(h):
                cols = slice(h * CHUNK, (h + 1) * CHUNK)
                for t in range(PACK):
                    rows = slice(t * P, (t + 1) * P)
                    y_bank = banks.tile([P, CHUNK], F32, tag="num_t")
                    nc.tensor.matmul_mx(
                        out=y_bank[:],
                        lhsT=w_codes["c1"][:, rows].bitcast(FP8X4),
                        lhsT_scale=w_scales["c1"][:, rows],
                        rhs=ll_codes[:, cols].bitcast(FP8X4),
                        rhs_scale=ll_scales[:, cols],
                        start=True,
                        stop=True,
                    )
                    nc.scalar.activation(
                        out=y_rows[:, t, cols], in_=y_bank[:], func=ACT.Identity, scale=0.5, bias=bias_c1[:, t : t + 1]
                    )

            def group_y(h):
                cols = slice(h * CHUNK, (h + 1) * CHUNK)
                nc.vector.tensor_copy(out=y_bf[:, cols, :], in_=y_rows[:, :, cols].rearrange("p t x -> p x t"))

            def quantise_y(h):
                cols = slice(h * CHUNK, (h + 1) * CHUNK)
                nc.vector.quantize_mx(
                    out=y_codes[:, cols].bitcast(FP8X4),
                    scales=y_scales[:, cols],
                    in_=y_bf[:, cols, :].rearrange("p x t -> p (x t)"),
                )

            turn_weight("c1")
            nc.scalar.copy(out=bias_c1[:], in_=b1_bf[:])
            add_rows(0)
            add_columns(0)
            add_rows(1)
            quantise_ll(0)
            quantise_weight("c1")
            add_columns(1)
            add_rows(2)
            quantise_ll(1)
            turn_weight("q")
            first_convolution(0)
            turn_weight("k")
            turn_weight("v")
            add_columns(2)
            add_rows(3)
            quantise_ll(2)
            add_columns(3)
            quantise_weight("q")
            quantise_ll(3)
            first_convolution(1)
            group_y(0)
            quantise_weight("k")
            quantise_y(0)
            quantise_weight("v")
            group_y(1)
            quantise_y(1)

        z_pair = (z_even, z_odd)
        pv_blocks = pv[:].rearrange("p s t b (f i) j -> p (s t) (b f) (i j)", f=2)
        out_tiles = out.rearrange("b (r a) h w -> a r b (h w)", a=TILES)
        q_of, k_of, v_of, e_of, den_of, num_of = {}, {}, {}, {}, {}, {}
        r_den_of, att_of, sums_of, mean_of, var_of, r_std_of, above_of, below_of = {}, {}, {}, {}, {}, {}, {}, {}

        with tc.tile_pool(name="work", bufs=2) as work:

            def project(name, c, tag, bufs):
                a, h = divmod(c, HALVES)
                bank = banks.tile([P, PAIR, SIDE, SIDE], F32, tag=tag, bufs=bufs)
                rows = slice(a * P, (a + 1) * P)
                cols = slice(h * CHUNK, (h + 1) * CHUNK)
                nc.tensor.matmul_mx(
                    out=bank[:].rearrange("p b i j -> p (b i j)"),
                    lhsT=w_codes[name][:, rows].bitcast(FP8X4),
                    lhsT_scale=w_scales[name][:, rows],
                    rhs=y_codes[:, cols].bitcast(FP8X4),
                    rhs_scale=y_scales[:, cols],
                    start=True,
                    stop=True,
                )
                return bank

            def project_qk(c):
                q_bank = project("q", c, "short", 2)
                k_of[c] = project("k", c, "bank_k", 1)
                q_sb = work.tile([P, PAIR, SIDE, SIDE], F32, tag="q_sb")
                nc.scalar.copy(out=q_sb[:], in_=q_bank[:])
                q_of[c] = q_sb

            def project_v(c):
                v_of[c] = project("v", c, "bank_v", 1)

            def times_neighbours(planes, bank, maps):
                for s, di in enumerate(SHIFTS):
                    i0, i1 = inside(di)
                    for t, dj in enumerate(SHIFTS):
                        j0, j1 = inside(dj)
                        nc.vector.tensor_tensor(
                            out=planes[:, s, t, :, i0:i1, j0:j1],
                            in0=bank[:, :, i0 + di : i1 + di, j0 + dj : j1 + dj],
                            in1=maps(s, t)[:, :, i0:i1, j0:j1],
                            op=ALU.mult,
                        )

            def sum_planes(blocks, tag):
                total = banks.tile([P, BLOCKS, P], F32, tag=tag)
                for g in range(BLOCKS):
                    for d in range(TAPS):
                        nc.tensor.matmul(
                            out=total[:, g, :],
                            lhsT=blocks[:, d, g, :],
                            rhs=ident[:],
                            is_transpose=True,
                            start=(d == 0),
                            stop=(d == TAPS - 1),
                        )
                return total

            def products(c):
                times_neighbours(z_pair[c % 2], k_of[c], lambda s, t: q_of[c])

            def stabilise(c):
                z_planes = z_pair[c % 2][:].rearrange("p s t b i j -> p (s t) b (i j)")
                top = work.tile([P, 4, PAIR, PIX], F32, tag="top")
                z_max = work.tile([P, PAIR, PIX], F32, tag="z_max")
                for b in range(PAIR):
                    nc.vector.tensor_max(out=top[:, :, b], in0=z_planes[:, 0:4, b], in1=z_planes[:, 4:8, b])
                for b in range(PAIR):
                    nc.vector.tensor_max(out=top[:, 0:2, b], in0=top[:, 0:2, b], in1=top[:, 2:4, b])
                for b in range(PAIR):
                    nc.vector.tensor_max(out=top[:, 0, b], in0=top[:, 0, b], in1=top[:, 1, b])
                for b in range(PAIR):
                    nc.vector.tensor_max(out=z_max[:, b], in0=top[:, 0, b], in1=z_planes[:, 8, b])
                e = work.tile([P, TAPS, PAIR, PIX], F32, tag="e")
                for b in range(PAIR):
                    idle_vector = c == CHUNKS - 1 or (c == 0 and b == PAIR - 1)
                    subtractor = nc.vector if idle_vector else nc.gpsimd
                    subtractor.tensor_tensor(
                        out=e[:, :, b],
                        in0=z_planes[:, :, b],
                        in1=z_max[:, b].unsqueeze(1).to_broadcast([P, TAPS, PIX]),
                        op=ALU.subtract,
                    )
                    nc.scalar.activation(out=e[:, :, b], in_=e[:, :, b], func=ACT.Exp)
                e_of[c] = e

            def sum_e(c):
                den_of[c] = sum_planes(e_of[c][:].rearrange("p d b (f x) -> p d (b f) x", f=2), "den_t")

            def weigh(c):
                e_maps = e_of[c][:].rearrange("p (s t) b (i j) -> p s t b i j", s=len(SHIFTS), i=SIDE)
                times_neighbours(pv, v_of[c], lambda s, t: e_maps[:, s, t])
                num_of[c] = sum_planes(pv_blocks, "num_t")

            def reciprocal(a):
                ln_den = work.tile([P, HALVES, BLOCKS, P], F32, tag="ln_den", bufs=1)
                for h in range(HALVES):
                    nc.scalar.activation(out=ln_den[:, h], in_=den_of[a * HALVES + h][:], func=ACT.Ln)
                r_den = work.tile([P, HALVES, BLOCKS, P], F32, tag="r_den")
                nc.scalar.activation(out=r_den[:], in_=ln_den[:], func=ACT.Exp, scale=-1.0)
                r_den_of[a] = r_den

            def divide(a):
                att = work.tile([P, HALVES, CHUNK], F32, tag="att")
                att_sums = work.tile([P, HALVES], F32, tag="att_sums")
                for h in range(HALVES):
                    att_t = work.tile([P, BLOCKS, P], F32, tag="att_t")
                    nc.vector.tensor_mul(out=att_t[:], in0=num_of[a * HALVES + h][:], in1=r_den_of[a][:, h])
                    att_bank = banks.tile([P, BLOCKS, P], F32, tag="short")
                    for g in range(BLOCKS):
                        nc.tensor.transpose(att_bank[:, g, :], att_t[:, g, :], ident[:])
                    nc.scalar.activation(
                        out=att[:, h, :],
                        in_=att_bank[:].rearrange("p g x -> p (g x)"),
                        func=ACT.Copy,
                        accum_out=att_sums[:, h : h + 1],
                    )
                att_of[a], sums_of[a] = att, att_sums

            def statistics(a):
                parts = work.tile([P, HALVES], F32, tag="parts")
                nc.scalar.activation(out=parts[:], in_=sums_of[a][:], func=ACT.Copy, scale=-1.0 / BN_COUNT)
                minus_mean = work.tile([P, 1], F32, tag="minus_mean")
                nc.scalar.activation(out=minus_mean[:], in_=parts[:, 0:1], func=ACT.Identity, bias=parts[:, 1:2])
                squares = work.tile([P, HALVES * CHUNK], F32, tag="squares", bufs=1)
                sum_squares = work.tile([P, 1], F32, tag="sum_squares")
                nc.scalar.activation(
                    out=squares[:],
                    in_=att_of[a][:].rearrange("p h x -> p (h x)"),
                    func=ACT.Square,
                    bias=minus_mean[:],
                    accum_out=sum_squares[:],
                )
                var_eps = work.tile([P, 1], F32, tag="var_eps")
                nc.scalar.activation(
                    out=var_eps[:], in_=sum_squares[:], func=ACT.Identity, scale=1.0 / BN_COUNT, bias=eps[:]
                )
                mean_of[a], var_of[a] = minus_mean, var_eps

            def rsqrt(a):
                r_std = work.tile([P, 1], F32, tag="r_std")
                nc.gpsimd.tensor_tensor(out=r_std[:], in0=var_of[a][:], in1=minus_half[:], op=ALU.pow)
                r_std_of[a] = r_std

            def affine(a):
                gain = work.tile([P, 2], F32, tag="gain")
                nc.scalar.activation(out=gain[:], in_=gamma_pm[:, a, :], func=ACT.Copy, scale=r_std_of[a][:])
                shift = work.tile([P, 2], F32, tag="shift")
                for sign in range(2):
                    nc.scalar.activation(
                        out=shift[:, sign : sign + 1],
                        in_=gain[:, sign : sign + 1],
                        func=ACT.Identity,
                        scale=mean_of[a][:],
                        bias=beta_pm[:, a, sign : sign + 1],
                    )
                above = work.tile([P, HALVES, CHUNK], F32, tag="above")
                below = work.tile([P, HALVES, CHUNK], F32, tag="below")
                for h in range(HALVES):
                    nc.scalar.activation(
                        out=above[:, h], in_=att_of[a][:, h], func=ACT.Relu, scale=gain[:, 0:1], bias=shift[:, 0:1]
                    )
                    nc.scalar.activation(
                        out=below[:, h], in_=att_of[a][:, h], func=ACT.Relu, scale=gain[:, 1:2], bias=shift[:, 1:2]
                    )
                above_of[a], below_of[a] = above, below

            def finish(a):
                result = work.tile([P, HALVES, CHUNK], F32, tag="result")
                for h in range(HALVES):
                    nc.vector.scalar_tensor_tensor(
                        out=result[:, h],
                        in0=below_of[a][:, h],
                        scalar=minus_slope[:],
                        in1=above_of[a][:, h],
                        op0=ALU.mult,
                        op1=ALU.add,
                    )
                    nc.sync.dma_start(
                        out=out_tiles[a][:, h * PAIR : (h + 1) * PAIR, :],
                        in_=result[:, h].rearrange("p (b x) -> p b x", b=PAIR),
                    )

            def live(c):
                return 0 <= c < CHUNKS

            def group_due(r, lag):
                a, rest = divmod(r - lag, HALVES)
                return a if rest == 0 and 0 <= a < TILES else None

            project_qk(0)
            nc.scalar.copy(out=gamma_pm[:, :, 0], in_=gamma_bf[:])
            nc.scalar.mul(out=gamma_pm[:, :, 1], in_=gamma_bf[:], mul=-1.0)
            nc.scalar.copy(out=beta_pm[:, :, 0], in_=beta_bf[:])
            nc.scalar.mul(out=beta_pm[:, :, 1], in_=beta_bf[:], mul=-1.0)
            nc.scalar.mul(out=minus_slope[:], in_=slope_bf[:], mul=-1.0)
            for r in range(CHUNKS + 4):
                if live(r):
                    products(r)
                if live(r + 1):
                    project_qk(r + 1)
                if group_due(r, 3) is not None:
                    divide(group_due(r, 3))
                    statistics(group_due(r, 3))
                if live(r - 1):
                    sum_e(r - 1)
                if group_due(r, 4) is not None:
                    affine(group_due(r, 4))
                if group_due(r, 2) is not None:
                    reciprocal(group_due(r, 2))
                if group_due(r, 5) is not None:
                    finish(group_due(r, 5))
                if live(r):
                    stabilise(r)
                if live(r - 1):
                    weigh(r - 1)
                if live(r):
                    project_v(r)
                if group_due(r, 3) is not None:
                    rsqrt(group_due(r, 3))
